import numpy as np
import ml_dtypes


def mxq(x, axis, fmt="e4m3"):
    dtype, down = {"e4m3": (ml_dtypes.float8_e4m3fn, 7), "e5m2": (ml_dtypes.float8_e5m2, 14)}[fmt]
    v = np.moveaxis(np.asarray(x, np.float32).astype(ml_dtypes.bfloat16).astype(np.float64), axis, -1)
    blocks = v.reshape(v.shape[:-1] + (-1, 32))
    amax = np.abs(blocks).max(-1, keepdims=True)
    byte = np.maximum(np.where(amax > 0, np.frexp(amax)[1] - 1 + 127, 0) - down, 1)
    scale = np.exp2(byte - 127.0)
    codes = (blocks / scale).astype(np.float32).astype(dtype).astype(np.float64)
    return np.moveaxis((codes * scale).reshape(v.shape), -1, axis)


WIDE = False


def mx_kscale(k):
    if not WIDE:
        return np.ones(k)
    levels = np.array([10, -10, 5, -5, 0])
    a = np.random.permutation(np.resize(levels, k // 512 * 4)).reshape(k // 512, 4)
    idx = np.arange(k)
    return np.exp2(a[idx // 512, idx % 128 // 32])


BF16 = ml_dtypes.bfloat16


def bf(x):
    return np.asarray(x, np.float32).astype(BF16)


def f64(x):
    return np.asarray(x).astype(np.float64)


B, L, D, H = 1, 4096, 512, 2
LN_EPS = 1e-5


def setup_inputs():
    s = mx_kscale(H * D)
    return {"heads": bf(np.random.standard_normal((H, L, D)) * 0.25 * s.reshape(H, D)[:, None, :]),
            "q": bf(np.random.standard_normal((B, L, D))),
            "proj_w": bf(np.random.standard_normal((D, H * D)) * 4.0 / np.sqrt(H * D) / s[None, :]),
            "proj_b": bf(np.random.standard_normal(D) * 0.1),
            "ln_gamma": bf(1.0 + np.random.standard_normal(D) * 0.1),
            "ln_beta": bf(np.random.standard_normal(D) * 0.1)}


def reference(heads, q, proj_w, proj_b, ln_gamma, ln_beta):
    hc = f64(heads).transpose(1, 0, 2).reshape(B, L, H * D)
    o = (mxq(hc, 2, "e4m3") @ mxq(f64(proj_w), 1, "e4m3").T) + f64(proj_b)
    x = o + f64(q)
    mu = x.mean(-1, keepdims=True)
    var = ((x - mu) ** 2).mean(-1, keepdims=True)
    return (x - mu) / np.sqrt(var + LN_EPS) * f64(ln_gamma) + f64(ln_beta)

@@ -1,0 +1,271 @@
+from contextlib import ExitStack
+
+import concourse.mybir as mybir
+from concourse.masks import make_identity
+
+F32 = mybir.dt.float32
+BF16 = mybir.dt.bfloat16
+U32 = mybir.dt.uint32
+U8 = mybir.dt.uint8
+FP8X4 = mybir.dt.float8_e4m3fn_x4
+ALU = mybir.AluOpType
+ACT = mybir.ActivationFunctionType
+
+P = 128
+HEADS = 2
+D = 512
+ROWS = 4096
+PACK = 4
+HALVES = 2
+TILES = 2
+UNITS_PER_GROUP = 2
+GROUP_TILES = TILES * UNITS_PER_GROUP
+GROUPS = ROWS // (P * GROUP_TILES)
+UNITS = GROUPS * UNITS_PER_GROUP
+W_TILES = D // P
+LN_EPS = 1e-5
+
+FLOPS = 2 * ROWS * HEADS * D * D
+
+
+def tile_multiheadattention_pb_t_kernel(
+    tc, heads, q, proj_w, proj_b, ln_gamma, ln_beta, out
+):
+    nc = tc.nc
+    heads_groups = heads.rearrange("h (g p t) d -> g p h (t d)", p=P, t=GROUP_TILES)
+    q_groups = q.flatten_outer_dims().rearrange("(g p t) d -> g p (t d)", p=P, t=GROUP_TILES)
+    out_groups = out.flatten_outer_dims().rearrange(
+        "(g p t) d -> g p (t d)", p=P, t=GROUP_TILES
+    )
+
+    with ExitStack() as stack:
+        const = stack.enter_context(tc.tile_pool(name="const", bufs=1))
+        heads_pool = stack.enter_context(tc.tile_pool(name="heads", bufs=3))
+        q_pool = stack.enter_context(tc.tile_pool(name="q", bufs=3))
+        resid_pool = stack.enter_context(tc.tile_pool(name="resid", bufs=4))
+        grouped_pool = stack.enter_context(tc.tile_pool(name="grouped", bufs=3))
+        mx_pool = stack.enter_context(tc.tile_pool(name="mx", bufs=3))
+        x_pool = stack.enter_context(tc.tile_pool(name="x", bufs=3))
+        y_pool = stack.enter_context(tc.tile_pool(name="y", bufs=4))
+        scratch_pool = stack.enter_context(tc.tile_pool(name="scratch", bufs=4))
+        stats_pool = stack.enter_context(tc.tile_pool(name="stats", bufs=4))
+        affine_psum = stack.enter_context(tc.psum_pool(name="affine_psum", bufs=1))
+        flip_psum = stack.enter_context(tc.psum_pool(name="flip_psum", bufs=3))
+        acc_psum = stack.enter_context(tc.psum_pool(name="acc_psum", bufs=2 * TILES))
+        stack.enter_context(tc.manual_schedule())
+
+        heads_sb, q_sb, resid, grouped, codes, scales = {}, {}, {}, {}, {}, {}
+        acc, x_sb, y_sb, row_sum, mean, rstd = {}, {}, {}, {}, {}, {}
+
+        def load(g, pieces):
+            heads_sb[g] = heads_pool.tile([P, HEADS, GROUP_TILES * D], BF16, name="heads_sb")
+            q_sb[g] = q_pool.tile([P, GROUP_TILES * D], BF16, name="q_sb")
+            width = GROUP_TILES * D // pieces
+            for piece in range(pieces):
+                cols = slice(piece * width, (piece + 1) * width)
+                nc.sync.dma_start(out=heads_sb[g][:, :, cols], in_=heads_groups[g][:, :, cols])
+                nc.sync.dma_start(out=q_sb[g][:, cols], in_=q_groups[g][:, cols])
+
+        def flip_rows(src_words, dst_words, copy):
+            flipped = flip_psum.tile([P, HEADS * HALVES * P], F32, tag="flipped")
+            planes = flipped[:].rearrange("p (h u r) -> p h u r", h=HEADS, u=HALVES)
+            for h in range(HEADS):
+                for u in range(HALVES):
+                    nc.tensor.transpose(planes[:, h, u, :], src_words[:, h, u, :], ident[:])
+            copy(out=dst_words, in_=planes.rearrange("p h u r -> p h r u"))
+
+        def flip_unit(unit):
+            g, part = divmod(unit, UNITS_PER_GROUP)
+            src = (
+                heads_sb[g][:]
+                .rearrange("p h x -> p (h x)")
+                .bitcast(F32)
+                .rearrange("p (h t u w) -> p h t u w", h=HEADS, t=GROUP_TILES, u=HALVES)
+            )
+            grouped[unit] = grouped_pool.tile(
+                [P, TILES * HEADS * P * PACK], BF16, name="grouped", align_bytes=64
+            )
+            dst = grouped[unit][:].bitcast(F32).rearrange(
+                "p (t h r u) -> p t h r u", t=TILES, h=HEADS, u=HALVES
+            )
+            for t in range(TILES):
+                flip_rows(src[:, :, part * TILES + t], dst[:, t], nc.scalar.copy)
+
+        def add_bias(unit):
+            g, part = divmod(unit, UNITS_PER_GROUP)
+            resid[unit] = resid_pool.tile([P, TILES, D], F32, name="resid")
+            nc.gpsimd.tensor_tensor(
+                out=resid[unit][:],
+                in0=q_sb[g][:, part * TILES * D : (part + 1) * TILES * D].rearrange(
+                    "p (t n) -> p t n", t=TILES
+                ),
+                in1=bias_sb[:].unsqueeze(1).to_broadcast([P, TILES, D]),
+                op=ALU.add,
+            )
+
+        def quantise(unit):
+            codes[unit] = mx_pool.tile([P, TILES * HEADS * P], U32, name="codes", align_bytes=64)
+            scales[unit] = mx_pool.tile([P, TILES * HEADS * P], U8, name="scales", align_bytes=64)
+            nc.vector.quantize_mx(
+                out=codes[unit][:].bitcast(FP8X4), scales=scales[unit][:], in_=grouped[unit][:]
+            )
+
+        def project(unit):
+            for t in range(TILES):
+                acc[unit, t] = acc_psum.tile([P, D], F32, name="acc")
+                for h in range(HEADS):
+                    rows = slice((t * HEADS + h) * P, (t * HEADS + h + 1) * P)
+                    cols = slice(h * D, (h + 1) * D)
+                    nc.tensor.matmul_mx(
+                        out=acc[unit, t][:],
+                        lhsT=codes[unit][:, rows].bitcast(FP8X4),
+                        lhsT_scale=scales[unit][:, rows],
+                        rhs=w_codes[:, cols].bitcast(FP8X4),
+                        rhs_scale=w_scales[:, cols],
+                        start=(h == 0),
+                        stop=(h == HEADS - 1),
+                    )
+
+        def add_residual(unit):
+            x_sb[unit] = x_pool.tile([P, TILES, D], F32, name="x_sb")
+            row_sum[unit] = stats_pool.tile([P, TILES], F32, name="row_sum")
+            for t in range(TILES):
+                nc.vector.scalar_tensor_tensor(
+                    out=x_sb[unit][:, t, :],
+                    in0=acc[unit, t][:],
+                    scalar=1.0,
+                    in1=resid[unit][:, t, :],
+                    op0=ALU.mult,
+                    op1=ALU.add,
+                    accum_out=row_sum[unit][:, t : t + 1],
+                )
+
+        def statistics(unit):
+            mean[unit] = stats_pool.tile([P, TILES], F32, name="mean")
+            nc.scalar.mul(out=mean[unit][:], in_=row_sum[unit][:], mul=1.0 / D)
+            sq_sum = stats_pool.tile([P, TILES], F32, name="sq_sum")
+            for t in range(TILES):
+                squares = scratch_pool.tile([P, D], BF16, name="squares")
+                nc.scalar.activation(
+                    out=squares[:],
+                    in_=x_sb[unit][:, t, :],
+                    func=ACT.Square,
+                    bias=mean[unit][:, t : t + 1],
+                    scale=-1.0,
+                    accum_out=sq_sum[:, t : t + 1],
+                )
+            rstd[unit] = stats_pool.tile([P, TILES], F32, name="rstd")
+            nc.scalar.activation(
+                out=rstd[unit][:],
+                in_=sq_sum[:],
+                func=ACT.Abs_reciprocal_sqrt,
+                bias=eps[:],
+                scale=1.0 / D,
+            )
+
+        def centre(unit):
+            y_sb[unit] = y_pool.tile([P, TILES, D], F32, name="y_sb")
+            for t in range(TILES):
+                nc.vector.scalar_tensor_tensor(
+                    out=y_sb[unit][:, t, :],
+                    in0=x_sb[unit][:, t, :],
+                    scalar=mean[unit][:, t : t + 1],
+                    in1=gamma_bc,
+                    op0=ALU.subtract,
+                    op1=ALU.mult,
+                )
+
+        def finish(unit):
+            g, part = divmod(unit, UNITS_PER_GROUP)
+            for t in range(TILES):
+                nc.vector.scalar_tensor_tensor(
+                    out=y_sb[unit][:, t, :],
+                    in0=y_sb[unit][:, t, :],
+                    scalar=rstd[unit][:, t : t + 1],
+                    in1=beta_bc,
+                    op0=ALU.mult,
+                    op1=ALU.add,
+                )
+            nc.sync.dma_start(
+                out=out_groups[g][:, part * TILES * D : (part + 1) * TILES * D],
+                in_=y_sb[unit][:].rearrange("p t n -> p (t n)"),
+            )
+
+        ident = const.tile([P, P], F32)
+        make_identity(nc, ident[:])
+        ones = const.tile([P, P], BF16)
+        nc.vector.memset(ones[:], 1.0)
+        eps = const.tile([P, 1], F32)
+        nc.vector.memset(eps[:], LN_EPS)
+        vec_rows = const.tile([P, 3 * D], BF16)
+        nc.vector.memset(vec_rows[:], 0.0)
+        warm = const.tile([P, 1], F32)
+        nc.scalar.activation(out=warm[:], in_=eps[:], func=ACT.Abs_reciprocal_sqrt)
+
+        w_raw = const.tile([P, W_TILES, HEADS * D], BF16)
+        w_rows = proj_w.rearrange("(j p) k -> p j k", p=P)
+        for half in range(2):
+            js = slice(half * W_TILES // 2, (half + 1) * W_TILES // 2)
+            nc.sync.dma_start(out=w_raw[:, js, :], in_=w_rows[:, js, :])
+        for i, vec in enumerate((proj_b, ln_gamma, ln_beta)):
+            nc.sync.dma_start(out=vec_rows[0:1, i * D : (i + 1) * D], in_=vec.unsqueeze(0))
+        load(0, pieces=UNITS_PER_GROUP)
+        load(1, pieces=1)
+
+        w_words = (
+            w_raw[:]
+            .rearrange("p j k -> p (j k)")
+            .bitcast(F32)
+            .rearrange("p (j h u w) -> p j h u w", j=W_TILES, h=HEADS, u=HALVES)
+        )
+        w_grouped = const.tile([P, HEADS * D * PACK], BF16, align_bytes=64)
+        w_grouped_words = w_grouped[:].bitcast(F32).rearrange(
+            "p (h n u) -> p h n u", h=HEADS, u=HALVES
+        )
+        for j in range(W_TILES):
+            flip_rows(
+                w_words[:, j],
+                w_grouped_words[:, :, j * P : (j + 1) * P, :],
+                nc.vector.tensor_copy if j % 2 == 0 else nc.scalar.copy,
+            )
+
+        bias_ps = flip_psum.tile([P, D], F32, tag="flipped")
+        nc.tensor.matmul(out=bias_ps[:], lhsT=ones[:], rhs=vec_rows[:, 0:D], start=True, stop=True)
+        bias_sb = const.tile([P, D], F32)
+        nc.vector.tensor_copy(out=bias_sb[:], in_=bias_ps[:])
+        affine = affine_psum.tile([P, 2 * D], BF16)
+        for i in range(2):
+            nc.tensor.matmul(
+                out=affine[:, i * D : (i + 1) * D],
+                lhsT=ones[:],
+                rhs=vec_rows[:, (i + 1) * D : (i + 2) * D],
+                start=True,
+                stop=True,
+            )
+        gamma_bc = affine[:, 0:D]
+        beta_bc = affine[:, D : 2 * D]
+
+        w_codes = const.tile([P, HEADS * D], U32, align_bytes=64)
+        w_scales = const.tile([P, HEADS * D], U8, align_bytes=64)
+        nc.vector.quantize_mx(
+            out=w_codes[:].bitcast(FP8X4), scales=w_scales[:], in_=w_grouped[:]
+        )
+
+        for unit in range(-2, UNITS + 1):
+            ahead = unit + 2
+            if ahead % UNITS_PER_GROUP == 0 and ahead // UNITS_PER_GROUP + 2 < GROUPS:
+                load(ahead // UNITS_PER_GROUP + 2, pieces=1)
+            if ahead < UNITS:
+                flip_unit(ahead)
+                add_bias(ahead)
+            if 0 <= unit < UNITS:
+                add_residual(unit)
+            if 0 <= unit + 1 < UNITS:
+                quantise(unit + 1)
+                project(unit + 1)
+            if 0 <= unit < UNITS:
+                statistics(unit)
+            if 0 <= unit - 1:
+                finish(unit - 1)
+            if 0 <= unit < UNITS:
+                centre(unit)

@@ -42,7 +42,7 @@ def tile_multiheadattention_pb_t_kernel(
         const = stack.enter_context(tc.tile_pool(name="const", bufs=1))
         heads_pool = stack.enter_context(tc.tile_pool(name="heads", bufs=3))
         q_pool = stack.enter_context(tc.tile_pool(name="q", bufs=3))
-        resid_pool = stack.enter_context(tc.tile_pool(name="resid", bufs=4))
+        resid_pool = stack.enter_context(tc.tile_pool(name="resid", bufs=4 * TILES))
         grouped_pool = stack.enter_context(tc.tile_pool(name="grouped", bufs=3))
         mx_pool = stack.enter_context(tc.tile_pool(name="mx", bufs=3))
         x_pool = stack.enter_context(tc.tile_pool(name="x", bufs=3))
@@ -93,15 +93,15 @@ def tile_multiheadattention_pb_t_kernel(
 
         def add_bias(unit):
             g, part = divmod(unit, UNITS_PER_GROUP)
-            resid[unit] = resid_pool.tile([P, TILES, D], F32, name="resid")
-            nc.gpsimd.tensor_tensor(
-                out=resid[unit][:],
-                in0=q_sb[g][:, part * TILES * D : (part + 1) * TILES * D].rearrange(
-                    "p (t n) -> p t n", t=TILES
-                ),
-                in1=bias_sb[:].unsqueeze(1).to_broadcast([P, TILES, D]),
-                op=ALU.add,
-            )
+            for t in range(TILES):
+                first = (part * TILES + t) * D
+                resid[unit, t] = resid_pool.tile([P, D], F32, name="resid")
+                nc.gpsimd.tensor_tensor(
+                    out=resid[unit, t][:],
+                    in0=q_sb[g][:, first : first + D],
+                    in1=bias_sb[:],
+                    op=ALU.add,
+                )
 
         def quantise(unit):
             codes[unit] = mx_pool.tile([P, TILES * HEADS * P], U32, name="codes", align_bytes=64)
@@ -134,7 +134,7 @@ def tile_multiheadattention_pb_t_kernel(
                     out=x_sb[unit][:, t, :],
                     in0=acc[unit, t][:],
                     scalar=1.0,
-                    in1=resid[unit][:, t, :],
+                    in1=resid[unit, t][:],
                     op0=ALU.mult,
                     op1=ALU.add,
                     accum_out=row_sum[unit][:, t : t + 1],
@@ -258,12 +258,11 @@ def tile_multiheadattention_pb_t_kernel(
             if ahead < UNITS:
                 flip_unit(ahead)
                 add_bias(ahead)
-            if 0 <= unit < UNITS:
-                add_residual(unit)
             if 0 <= unit + 1 < UNITS:
                 quantise(unit + 1)
                 project(unit + 1)
             if 0 <= unit < UNITS:
+                add_residual(unit)
                 statistics(unit)
             if 0 <= unit - 1:
                 finish(unit - 1)

@@ -24,6 +24,8 @@ GROUPS = ROWS // (P * GROUP_TILES)
 UNITS = GROUPS * UNITS_PER_GROUP
 W_TILES = D // P
 LN_EPS = 1e-5
+MX_AHEAD = 2
+FLIP_AHEAD = MX_AHEAD + 1
 
 FLOPS = 2 * ROWS * HEADS * D * D
 
@@ -42,7 +44,7 @@ def tile_multiheadattention_pb_t_kernel(
         const = stack.enter_context(tc.tile_pool(name="const", bufs=1))
         heads_pool = stack.enter_context(tc.tile_pool(name="heads", bufs=3))
         q_pool = stack.enter_context(tc.tile_pool(name="q", bufs=3))
-        resid_pool = stack.enter_context(tc.tile_pool(name="resid", bufs=4 * TILES))
+        resid_pool = stack.enter_context(tc.tile_pool(name="resid", bufs=4))
         grouped_pool = stack.enter_context(tc.tile_pool(name="grouped", bufs=3))
         mx_pool = stack.enter_context(tc.tile_pool(name="mx", bufs=3))
         x_pool = stack.enter_context(tc.tile_pool(name="x", bufs=3))
@@ -93,15 +95,15 @@ def tile_multiheadattention_pb_t_kernel(
 
         def add_bias(unit):
             g, part = divmod(unit, UNITS_PER_GROUP)
-            for t in range(TILES):
-                first = (part * TILES + t) * D
-                resid[unit, t] = resid_pool.tile([P, D], F32, name="resid")
-                nc.gpsimd.tensor_tensor(
-                    out=resid[unit, t][:],
-                    in0=q_sb[g][:, first : first + D],
-                    in1=bias_sb[:],
-                    op=ALU.add,
-                )
+            resid[unit] = resid_pool.tile([P, TILES, D], F32, name="resid")
+            nc.gpsimd.tensor_tensor(
+                out=resid[unit][:],
+                in0=q_sb[g][:, part * TILES * D : (part + 1) * TILES * D].rearrange(
+                    "p (t n) -> p t n", t=TILES
+                ),
+                in1=bias_sb[:].unsqueeze(1).to_broadcast([P, TILES, D]),
+                op=ALU.add,
+            )
 
         def quantise(unit):
             codes[unit] = mx_pool.tile([P, TILES * HEADS * P], U32, name="codes", align_bytes=64)
@@ -132,9 +134,9 @@ def tile_multiheadattention_pb_t_kernel(
             for t in range(TILES):
                 nc.vector.scalar_tensor_tensor(
                     out=x_sb[unit][:, t, :],
-                    in0=acc[unit, t][:],
+                    in0=resid[unit][:, t, :],
                     scalar=1.0,
-                    in1=resid[unit, t][:],
+                    in1=acc[unit, t][:],
                     op0=ALU.mult,
                     op1=ALU.add,
                     accum_out=row_sum[unit][:, t : t + 1],
@@ -251,18 +253,20 @@ def tile_multiheadattention_pb_t_kernel(
             out=w_codes[:].bitcast(FP8X4), scales=w_scales[:], in_=w_grouped[:]
         )
 
-        for unit in range(-2, UNITS + 1):
-            ahead = unit + 2
-            if ahead % UNITS_PER_GROUP == 0 and ahead // UNITS_PER_GROUP + 2 < GROUPS:
-                load(ahead // UNITS_PER_GROUP + 2, pieces=1)
-            if ahead < UNITS:
-                flip_unit(ahead)
-                add_bias(ahead)
-            if 0 <= unit + 1 < UNITS:
-                quantise(unit + 1)
-                project(unit + 1)
+        for unit in range(-FLIP_AHEAD, UNITS + 1):
+            flipped_unit = unit + FLIP_AHEAD
+            g, part = divmod(flipped_unit, UNITS_PER_GROUP)
+            if part == 0 and g + 2 < GROUPS:
+                load(g + 2, pieces=1)
+            if flipped_unit < UNITS:
+                flip_unit(flipped_unit)
+                add_bias(flipped_unit)
             if 0 <= unit < UNITS:
                 add_residual(unit)
+            if 0 <= unit + MX_AHEAD < UNITS:
+                quantise(unit + MX_AHEAD)
+                project(unit + MX_AHEAD)
+            if 0 <= unit < UNITS:
                 statistics(unit)
             if 0 <= unit - 1:
                 finish(unit - 1)

from contextlib import ExitStack

import concourse.mybir as mybir
from concourse.masks import make_identity

F32 = mybir.dt.float32
BF16 = mybir.dt.bfloat16
U32 = mybir.dt.uint32
U8 = mybir.dt.uint8
FP8X4 = mybir.dt.float8_e4m3fn_x4
ALU = mybir.AluOpType
ACT = mybir.ActivationFunctionType

P = 128
HEADS = 2
D = 512
ROWS = 4096
PACK = 4
HALVES = 2
TILES = 2
UNITS_PER_GROUP = 2
GROUP_TILES = TILES * UNITS_PER_GROUP
GROUPS = ROWS // (P * GROUP_TILES)
UNITS = GROUPS * UNITS_PER_GROUP
W_TILES = D // P
LN_EPS = 1e-5
MX_AHEAD = 2
FLIP_AHEAD = MX_AHEAD + 1

FLOPS = 2 * ROWS * HEADS * D * D


def tile_multiheadattention_pb_t_kernel(
    tc, heads, q, proj_w, proj_b, ln_gamma, ln_beta, out
):
    nc = tc.nc
    heads_groups = heads.rearrange("h (g p t) d -> g p h (t d)", p=P, t=GROUP_TILES)
    q_groups = q.flatten_outer_dims().rearrange("(g p t) d -> g p (t d)", p=P, t=GROUP_TILES)
    out_groups = out.flatten_outer_dims().rearrange(
        "(g p t) d -> g p (t d)", p=P, t=GROUP_TILES
    )

    with ExitStack() as stack:
        const = stack.enter_context(tc.tile_pool(name="const", bufs=1))
        heads_pool = stack.enter_context(tc.tile_pool(name="heads", bufs=3))
        q_pool = stack.enter_context(tc.tile_pool(name="q", bufs=3))
        resid_pool = stack.enter_context(tc.tile_pool(name="resid", bufs=4))
        grouped_pool = stack.enter_context(tc.tile_pool(name="grouped", bufs=3))
        mx_pool = stack.enter_context(tc.tile_pool(name="mx", bufs=3))
        x_pool = stack.enter_context(tc.tile_pool(name="x", bufs=3))
        y_pool = stack.enter_context(tc.tile_pool(name="y", bufs=4))
        scratch_pool = stack.enter_context(tc.tile_pool(name="scratch", bufs=4))
        stats_pool = stack.enter_context(tc.tile_pool(name="stats", bufs=4))
        affine_psum = stack.enter_context(tc.psum_pool(name="affine_psum", bufs=1))
        flip_psum = stack.enter_context(tc.psum_pool(name="flip_psum", bufs=3))
        acc_psum = stack.enter_context(tc.psum_pool(name="acc_psum", bufs=2 * TILES))
        stack.enter_context(tc.manual_schedule())

        heads_sb, q_sb, resid, grouped, codes, scales = {}, {}, {}, {}, {}, {}
        acc, x_sb, y_sb, row_sum, mean, rstd = {}, {}, {}, {}, {}, {}

        def load(g, pieces):
            heads_sb[g] = heads_pool.tile([P, HEADS, GROUP_TILES * D], BF16, name="heads_sb")
            q_sb[g] = q_pool.tile([P, GROUP_TILES * D], BF16, name="q_sb")
            width = GROUP_TILES * D // pieces
            for piece in range(pieces):
                cols = slice(piece * width, (piece + 1) * width)
                nc.sync.dma_start(out=heads_sb[g][:, :, cols], in_=heads_groups[g][:, :, cols])
                nc.sync.dma_start(out=q_sb[g][:, cols], in_=q_groups[g][:, cols])

        def flip_rows(src_words, dst_words, copy):
            flipped = flip_psum.tile([P, HEADS * HALVES * P], F32, tag="flipped")
            planes = flipped[:].rearrange("p (h u r) -> p h u r", h=HEADS, u=HALVES)
            for h in range(HEADS):
                for u in range(HALVES):
                    nc.tensor.transpose(planes[:, h, u, :], src_words[:, h, u, :], ident[:])
            copy(out=dst_words, in_=planes.rearrange("p h u r -> p h r u"))

        def flip_unit(unit):
            g, part = divmod(unit, UNITS_PER_GROUP)
            src = (
                heads_sb[g][:]
                .rearrange("p h x -> p (h x)")
                .bitcast(F32)
                .rearrange("p (h t u w) -> p h t u w", h=HEADS, t=GROUP_TILES, u=HALVES)
            )
            grouped[unit] = grouped_pool.tile(
                [P, TILES * HEADS * P * PACK], BF16, name="grouped", align_bytes=64
            )
            dst = grouped[unit][:].bitcast(F32).rearrange(
                "p (t h r u) -> p t h r u", t=TILES, h=HEADS, u=HALVES
            )
            for t in range(TILES):
                flip_rows(src[:, :, part * TILES + t], dst[:, t], nc.scalar.copy)

        def add_bias(unit):
            g, part = divmod(unit, UNITS_PER_GROUP)
            resid[unit] = resid_pool.tile([P, TILES, D], F32, name="resid")
            nc.gpsimd.tensor_tensor(
                out=resid[unit][:],
                in0=q_sb[g][:, part * TILES * D : (part + 1) * TILES * D].rearrange(
                    "p (t n) -> p t n", t=TILES
                ),
                in1=bias_sb[:].unsqueeze(1).to_broadcast([P, TILES, D]),
                op=ALU.add,
            )

        def quantise(unit):
            codes[unit] = mx_pool.tile([P, TILES * HEADS * P], U32, name="codes", align_bytes=64)
            scales[unit] = mx_pool.tile([P, TILES * HEADS * P], U8, name="scales", align_bytes=64)
            nc.vector.quantize_mx(
                out=codes[unit][:].bitcast(FP8X4), scales=scales[unit][:], in_=grouped[unit][:]
            )

        def project(unit):
            for t in range(TILES):
                acc[unit, t] = acc_psum.tile([P, D], F32, name="acc")
                for h in range(HEADS):
                    rows = slice((t * HEADS + h) * P, (t * HEADS + h + 1) * P)
                    cols = slice(h * D, (h + 1) * D)
                    nc.tensor.matmul_mx(
                        out=acc[unit, t][:],
                        lhsT=codes[unit][:, rows].bitcast(FP8X4),
                        lhsT_scale=scales[unit][:, rows],
                        rhs=w_codes[:, cols].bitcast(FP8X4),
                        rhs_scale=w_scales[:, cols],
                        start=(h == 0),
                        stop=(h == HEADS - 1),
                    )

        def add_residual(unit):
            x_sb[unit] = x_pool.tile([P, TILES, D], F32, name="x_sb")
            row_sum[unit] = stats_pool.tile([P, TILES], F32, name="row_sum")
            for t in range(TILES):
                nc.vector.scalar_tensor_tensor(
                    out=x_sb[unit][:, t, :],
                    in0=resid[unit][:, t, :],
                    scalar=1.0,
                    in1=acc[unit, t][:],
                    op0=ALU.mult,
                    op1=ALU.add,
                    accum_out=row_sum[unit][:, t : t + 1],
                )

        def statistics(unit):
            mean[unit] = stats_pool.tile([P, TILES], F32, name="mean")
            nc.scalar.mul(out=mean[unit][:], in_=row_sum[unit][:], mul=1.0 / D)
            sq_sum = stats_pool.tile([P, TILES], F32, name="sq_sum")
            for t in range(TILES):
                squares = scratch_pool.tile([P, D], BF16, name="squares")
                nc.scalar.activation(
                    out=squares[:],
                    in_=x_sb[unit][:, t, :],
                    func=ACT.Square,
                    bias=mean[unit][:, t : t + 1],
                    scale=-1.0,
                    accum_out=sq_sum[:, t : t + 1],
                )
            rstd[unit] = stats_pool.tile([P, TILES], F32, name="rstd")
            nc.scalar.activation(
                out=rstd[unit][:],
                in_=sq_sum[:],
                func=ACT.Abs_reciprocal_sqrt,
                bias=eps[:],
                scale=1.0 / D,
            )

        def centre(unit):
            y_sb[unit] = y_pool.tile([P, TILES, D], F32, name="y_sb")
            for t in range(TILES):
                nc.vector.scalar_tensor_tensor(
                    out=y_sb[unit][:, t, :],
                    in0=x_sb[unit][:, t, :],
                    scalar=mean[unit][:, t : t + 1],
                    in1=gamma_bc,
                    op0=ALU.subtract,
                    op1=ALU.mult,
                )

        def finish(unit):
            g, part = divmod(unit, UNITS_PER_GROUP)
            for t in range(TILES):
                nc.vector.scalar_tensor_tensor(
                    out=y_sb[unit][:, t, :],
                    in0=y_sb[unit][:, t, :],
                    scalar=rstd[unit][:, t : t + 1],
                    in1=beta_bc,
                    op0=ALU.mult,
                    op1=ALU.add,
                )
            nc.sync.dma_start(
                out=out_groups[g][:, part * TILES * D : (part + 1) * TILES * D],
                in_=y_sb[unit][:].rearrange("p t n -> p (t n)"),
            )

        ident = const.tile([P, P], F32)
        make_identity(nc, ident[:])
        ones = const.tile([P, P], BF16)
        nc.vector.memset(ones[:], 1.0)
        eps = const.tile([P, 1], F32)
        nc.vector.memset(eps[:], LN_EPS)
        vec_rows = const.tile([P, 3 * D], BF16)
        nc.vector.memset(vec_rows[:], 0.0)
        warm = const.tile([P, 1], F32)
        nc.scalar.activation(out=warm[:], in_=eps[:], func=ACT.Abs_reciprocal_sqrt)

        w_raw = const.tile([P, W_TILES, HEADS * D], BF16)
        w_rows = proj_w.rearrange("(j p) k -> p j k", p=P)
        for half in range(2):
            js = slice(half * W_TILES // 2, (half + 1) * W_TILES // 2)
            nc.sync.dma_start(out=w_raw[:, js, :], in_=w_rows[:, js, :])
        for i, vec in enumerate((proj_b, ln_gamma, ln_beta)):
            nc.sync.dma_start(out=vec_rows[0:1, i * D : (i + 1) * D], in_=vec.unsqueeze(0))
        load(0, pieces=UNITS_PER_GROUP)
        load(1, pieces=1)

        w_words = (
            w_raw[:]
            .rearrange("p j k -> p (j k)")
            .bitcast(F32)
            .rearrange("p (j h u w) -> p j h u w", j=W_TILES, h=HEADS, u=HALVES)
        )
        w_grouped = const.tile([P, HEADS * D * PACK], BF16, align_bytes=64)
        w_grouped_words = w_grouped[:].bitcast(F32).rearrange(
            "p (h n u) -> p h n u", h=HEADS, u=HALVES
        )
        for j in range(W_TILES):
            flip_rows(
                w_words[:, j],
                w_grouped_words[:, :, j * P : (j + 1) * P, :],
                nc.vector.tensor_copy if j % 2 == 0 else nc.scalar.copy,
            )

        bias_ps = flip_psum.tile([P, D], F32, tag="flipped")
        nc.tensor.matmul(out=bias_ps[:], lhsT=ones[:], rhs=vec_rows[:, 0:D], start=True, stop=True)
        bias_sb = const.tile([P, D], F32)
        nc.vector.tensor_copy(out=bias_sb[:], in_=bias_ps[:])
        affine = affine_psum.tile([P, 2 * D], BF16)
        for i in range(2):
            nc.tensor.matmul(
                out=affine[:, i * D : (i + 1) * D],
                lhsT=ones[:],
                rhs=vec_rows[:, (i + 1) * D : (i + 2) * D],
                start=True,
                stop=True,
            )
        gamma_bc = affine[:, 0:D]
        beta_bc = affine[:, D : 2 * D]

        w_codes = const.tile([P, HEADS * D], U32, align_bytes=64)
        w_scales = const.tile([P, HEADS * D], U8, align_bytes=64)
        nc.vector.quantize_mx(
            out=w_codes[:].bitcast(FP8X4), scales=w_scales[:], in_=w_grouped[:]
        )

        for unit in range(-FLIP_AHEAD, UNITS + 1):
            flipped_unit = unit + FLIP_AHEAD
            g, part = divmod(flipped_unit, UNITS_PER_GROUP)
            if part == 0 and g + 2 < GROUPS:
                load(g + 2, pieces=1)
            if flipped_unit < UNITS:
                flip_unit(flipped_unit)
                add_bias(flipped_unit)
            if 0 <= unit < UNITS:
                add_residual(unit)
            if 0 <= unit + MX_AHEAD < UNITS:
                quantise(unit + MX_AHEAD)
                project(unit + MX_AHEAD)
            if 0 <= unit < UNITS:
                statistics(unit)
            if 0 <= unit - 1:
                finish(unit - 1)
            if 0 <= unit < UNITS:
                centre(unit)
